import numpy as np
import ml_dtypes


def mxq(x, axis, fmt="e4m3"):
    dtype, down = {"e4m3": (ml_dtypes.float8_e4m3fn, 7), "e5m2": (ml_dtypes.float8_e5m2, 14)}[fmt]
    v = np.moveaxis(np.asarray(x, np.float32).astype(ml_dtypes.bfloat16).astype(np.float64), axis, -1)
    blocks = v.reshape(v.shape[:-1] + (-1, 32))
    amax = np.abs(blocks).max(-1, keepdims=True)
    byte = np.maximum(np.where(amax > 0, np.frexp(amax)[1] - 1 + 127, 0) - down, 1)
    scale = np.exp2(byte - 127.0)
    codes = (blocks / scale).astype(np.float32).astype(dtype).astype(np.float64)
    return np.moveaxis((codes * scale).reshape(v.shape), -1, axis)


WIDE = False


def mx_kscale(k):
    if not WIDE:
        return np.ones(k)
    levels = np.array([10, -10, 5, -5, 0])
    a = np.random.permutation(np.resize(levels, k // 512 * 4)).reshape(k // 512, 4)
    idx = np.arange(k)
    return np.exp2(a[idx // 512, idx % 128 // 32])


BF16 = ml_dtypes.bfloat16


def bf(x):
    return np.asarray(x, np.float32).astype(BF16)


def f64(x):
    return np.asarray(x).astype(np.float64)


B, D, S, N = 1024, 2048, 4, 128
DS = D // S
EPS = 1e-12


def setup_inputs():
    s, t = mx_kscale(D), mx_kscale(D)
    return {"h": bf(np.random.standard_normal((B, D)) * s),
            "x2f": bf(np.random.standard_normal((B, D)) * t),
            "vu": bf(np.random.standard_normal((N, S, DS)) * 2.0 / np.sqrt(DS) / t.reshape(S, DS)),
            "w_f": bf(np.random.standard_normal((D, D)) / np.sqrt(D) * t[:, None] / s),
            "b_f": bf(np.random.standard_normal(D) * 0.2 * t),
            "bh": bf(1.0 + 0.1 * np.random.standard_normal(1)),
            "bx": bf(1.0 + 0.1 * np.random.standard_normal(1))}


def reference(h, x2f, vu, w_f, b_f, bh, bx):
    h2f = (mxq(f64(h), 1, "e4m3") @ mxq(f64(w_f), 1, "e4m3").T) + f64(b_f)
    vuq = mxq(f64(vu), 2, "e4m3").transpose(1, 2, 0)
    ah = (mxq(f64(x2f).reshape(B, S, DS), 2, "e4m3").transpose(1, 0, 2) @ vuq).transpose(1, 2, 0)
    ax = (mxq(h2f.reshape(B, S, DS), 2, "e4m3").transpose(1, 0, 2) @ vuq).transpose(1, 2, 0)
    ah = np.maximum(ah + f64(bh), 0.0)
    ax = np.maximum(ax + f64(bx), 0.0)
    a2 = (ah + ax) ** 2
    return a2 / np.maximum(a2.sum(axis=1, keepdims=True), EPS)

@@ -1,0 +1,201 @@
+from contextlib import ExitStack
+
+import concourse.mybir as mybir
+from concourse.masks import make_identity
+
+F32 = mybir.dt.float32
+BF16 = mybir.dt.bfloat16
+U32 = mybir.dt.uint32
+U8 = mybir.dt.uint8
+FP8X4 = mybir.dt.float8_e4m3fn_x4
+ACT = mybir.ActivationFunctionType
+ALU = mybir.AluOpType
+
+P = 128
+PACK = 4
+HALVES = 2
+K_PASS = P * PACK
+
+B, D, S, N = 1024, 2048, 4, 128
+DS = D // S
+PASSES = D // K_PASS
+ROW_TILES = B // P
+EPS = 1e-12
+
+FLOPS = 2 * B * D * D + 2 * (2 * B * D * N)
+
+
+def tile_tpru_pa_kernel(tc, h, x2f, vu, w_f, b_f, bh, bx, out):
+    nc = tc.nc
+    with ExitStack() as ctx:
+        keep = ctx.enter_context(tc.tile_pool(name="keep", bufs=1))
+        stage = ctx.enter_context(tc.tile_pool(name="stage", bufs=3))
+        work = ctx.enter_context(tc.tile_pool(name="work", bufs=2))
+        flip_psum = ctx.enter_context(tc.psum_pool(name="flip_psum", bufs=4))
+        feat_psum = ctx.enter_context(tc.psum_pool(name="feat_psum", bufs=2))
+        score_psum = ctx.enter_context(tc.psum_pool(name="score_psum", bufs=1))
+
+        w_rows = []
+        for s in range(S):
+            rows = keep.tile([P, PACK, D], BF16, name="w_rows%d" % s)
+            nc.sync.dma_start(
+                out=rows[:].rearrange("r (u e) k -> r u e k", u=HALVES),
+                in_=w_f[s * DS : (s + 1) * DS, :].rearrange("(u r e) k -> r u e k", u=HALVES, r=P),
+            )
+            w_rows.append(rows)
+            if s == 0:
+                vu_rows = keep.tile([P, D], BF16)
+                nc.sync.dma_start(out=vu_rows[:], in_=vu.rearrange("n s d -> n (s d)"))
+        h_rows = []
+        x_rows = []
+        for i in range(ROW_TILES):
+            rows = keep.tile([P, D], BF16, name="h_rows%d" % i)
+            nc.sync.dma_start(out=rows[:], in_=h[i * P : (i + 1) * P, :])
+            h_rows.append(rows)
+            rows = keep.tile([P, D], BF16, name="x_rows%d" % i)
+            nc.sync.dma_start(out=rows[:], in_=x2f[i * P : (i + 1) * P, :])
+            x_rows.append(rows)
+
+        ident = keep.tile([P, P], F32)
+        make_identity(nc, ident[:])
+        bias_bf = keep.tile([P, S, HALVES, 2], BF16)
+        nc.scalar.dma_start(
+            out=bias_bf[:], in_=b_f.rearrange("(s u p e) -> p s u e", s=S, u=HALVES, p=P)
+        )
+        bias = keep.tile([P, S, PACK], F32)
+        nc.vector.tensor_copy(out=bias[:], in_=bias_bf[:].rearrange("p s u e -> p s (u e)"))
+        bh_bf = keep.tile([P, 1], BF16)
+        nc.scalar.dma_start(out=bh_bf[:], in_=bh.partition_broadcast(P))
+        bh_all = keep.tile([P, 1], F32)
+        nc.vector.tensor_copy(out=bh_all[:], in_=bh_bf[:])
+        bx_bf = keep.tile([P, 1], BF16)
+        nc.scalar.dma_start(out=bx_bf[:], in_=bx.partition_broadcast(P))
+        bx_all = keep.tile([P, 1], F32)
+        nc.vector.tensor_copy(out=bx_all[:], in_=bx_bf[:])
+
+        def pack_rows(rows, codes, scales):
+            words = rows.bitcast(F32)
+            grouped = stage.tile([P, PASSES, P, HALVES], F32, align_bytes=64)
+            for first in range(0, PASSES, 2):
+                flipped = flip_psum.tile([P, 2, HALVES, P], F32)
+                for g in range(2):
+                    for u in range(HALVES):
+                        column = ((first + g) * HALVES + u) * P
+                        nc.tensor.transpose(
+                            flipped[:, g, u, :], words[:, column : column + P], ident[:]
+                        )
+                nc.scalar.copy(
+                    out=grouped[:, first : first + 2, :, :],
+                    in_=flipped[:].rearrange("q g u r -> q g r u"),
+                )
+            nc.vector.quantize_mx(
+                out=codes.rearrange("q g r -> q (g r)").bitcast(FP8X4),
+                scales=scales.rearrange("q g r -> q (g r)"),
+                in_=grouped[:].rearrange("q g r u -> q (g r u)").bitcast(BF16),
+            )
+
+        def pack_row_tile(i):
+            h_codes = stage.tile([P, PASSES, P], U32, align_bytes=64)
+            h_scales = stage.tile([P, PASSES, P], U8, align_bytes=64)
+            pack_rows(h_rows[i][:], h_codes[:], h_scales[:])
+            x_codes = stage.tile([P, S, P], U32, align_bytes=64)
+            x_scales = stage.tile([P, S, P], U8, align_bytes=64)
+            pack_rows(x_rows[i][:], x_codes[:], x_scales[:])
+            return h_codes, h_scales, x_codes, x_scales
+
+        vu_codes = keep.tile([P, S, N], U32, align_bytes=64)
+        vu_scales = keep.tile([P, S, N], U8, align_bytes=64)
+        w_codes = keep.tile([P, S, PACK, PASSES, P], U32, align_bytes=64)
+        w_scales = keep.tile([P, S, PACK, PASSES, P], U8, align_bytes=64)
+        for s in range(S):
+            for t in range(PACK):
+                pack_rows(w_rows[s][:, t, :], w_codes[:, s, t], w_scales[:, s, t])
+            if s == 0:
+                pack_rows(vu_rows[:], vu_codes[:], vu_scales[:])
+
+        packed = pack_row_tile(0)
+        for i in range(ROW_TILES):
+            h_codes, h_scales, x_codes, x_scales = packed
+            if i + 1 < ROW_TILES:
+                packed = pack_row_tile(i + 1)
+
+            ah = score_psum.tile([P, S, N], F32)
+            for s in range(S):
+                nc.tensor.matmul_mx(
+                    out=ah[:, s, :],
+                    lhsT=x_codes[:, s, :].bitcast(FP8X4),
+                    lhsT_scale=x_scales[:, s, :],
+                    rhs=vu_codes[:, s, :].bitcast(FP8X4),
+                    rhs_scale=vu_scales[:, s, :],
+                    start=True,
+                    stop=True,
+                )
+            relu_h = work.tile([P, S, N], F32)
+            nc.scalar.activation(out=relu_h[:], in_=ah[:], func=ACT.Relu, bias=bh_all[:], scale=1.0)
+
+            ax = score_psum.tile([P, S, N], F32)
+            for s in range(S):
+                feat = feat_psum.tile([P, PACK, P], F32)
+                for t in range(PACK):
+                    for g in range(PASSES):
+                        nc.tensor.matmul_mx(
+                            out=feat[:, t, :],
+                            lhsT=w_codes[:, s, t, g, :].bitcast(FP8X4),
+                            lhsT_scale=w_scales[:, s, t, g, :],
+                            rhs=h_codes[:, g, :].bitcast(FP8X4),
+                            rhs_scale=h_scales[:, g, :],
+                            start=(g == 0),
+                            stop=(g == PASSES - 1),
+                        )
+                f_grouped = stage.tile([P, P, PACK], BF16, align_bytes=64)
+                nc.vector.tensor_tensor(
+                    out=f_grouped[:],
+                    in0=feat[:].rearrange("p t b -> p b t"),
+                    in1=bias[:, s, :].unsqueeze(1).to_broadcast([P, P, PACK]),
+                    op=ALU.add,
+                )
+                f_codes = stage.tile([P, P], U32, align_bytes=64)
+                f_scales = stage.tile([P, P], U8, align_bytes=64)
+                nc.vector.quantize_mx(
+                    out=f_codes[:].bitcast(FP8X4),
+                    scales=f_scales[:],
+                    in_=f_grouped[:].rearrange("p b t -> p (b t)"),
+                )
+                nc.tensor.matmul_mx(
+                    out=ax[:, s, :],
+                    lhsT=f_codes[:].bitcast(FP8X4),
+                    lhsT_scale=f_scales[:],
+                    rhs=vu_codes[:, s, :].bitcast(FP8X4),
+                    rhs_scale=vu_scales[:, s, :],
+                    start=True,
+                    stop=True,
+                )
+            relu_x = work.tile([P, S, N], F32)
+            nc.scalar.activation(out=relu_x[:], in_=ax[:], func=ACT.Relu, bias=bx_all[:], scale=1.0)
+
+            both = work.tile([P, S, N], F32)
+            nc.vector.tensor_add(out=both[:], in0=relu_h[:], in1=relu_x[:])
+            squared = work.tile([P, S, N], F32)
+            total = work.tile([P, S], F32)
+            for s in range(S):
+                nc.scalar.activation(
+                    out=squared[:, s, :],
+                    in_=both[:, s, :],
+                    func=ACT.Square,
+                    accum_out=total[:, s : s + 1],
+                )
+            floored = work.tile([P, S], F32)
+            nc.vector.tensor_scalar_max(out=floored[:], in0=total[:], scalar1=EPS)
+            inverse = work.tile([P, S], F32)
+            nc.vector.reciprocal(out=inverse[:], in_=floored[:])
+            share = work.tile([P, N, S], F32)
+            nc.vector.tensor_tensor(
+                out=share[:],
+                in0=squared[:].rearrange("p s n -> p n s"),
+                in1=inverse[:].unsqueeze(1).to_broadcast([P, N, S]),
+                op=ALU.mult,
+            )
+            nc.sync.dma_start(
+                out=out[i * P : (i + 1) * P].rearrange("b n s -> b (n s)"),
+                in_=share[:].rearrange("p n s -> p (n s)"),
+            )

@@ -24,37 +24,59 @@ EPS = 1e-12
 
 FLOPS = 2 * B * D * D + 2 * (2 * B * D * N)
 
+EARLY = 3
+PACK_LEAD = 3
+SCORE_LAG = 3
+COMBINE_LAG = 4
+SQUARE_LAG = 5
+NORMALISE_LAG = 7
+
 
 def tile_tpru_pa_kernel(tc, h, x2f, vu, w_f, b_f, bh, bx, out):
     nc = tc.nc
+    units = [(i, s) for s in range(S) for i in range(EARLY)]
+    units += [(i, s) for i in range(EARLY, ROW_TILES) for s in range(S)]
+    steps = range(-(PACK_LEAD + 1), len(units) + NORMALISE_LAG)
+
+    def is_unit(k):
+        return 0 <= k < len(units)
+
     with ExitStack() as ctx:
         keep = ctx.enter_context(tc.tile_pool(name="keep", bufs=1))
-        stage = ctx.enter_context(tc.tile_pool(name="stage", bufs=3))
+        rows_pool = ctx.enter_context(tc.tile_pool(name="rows_pool", bufs=4))
+        flip_pool = ctx.enter_context(tc.tile_pool(name="flip_pool", bufs=6))
+        code_pool = ctx.enter_context(tc.tile_pool(name="code_pool", bufs=EARLY + 1))
+        feat_pool = ctx.enter_context(tc.tile_pool(name="feat_pool", bufs=4))
+        relu_pool = ctx.enter_context(tc.tile_pool(name="relu_pool", bufs=EARLY + 2))
         work = ctx.enter_context(tc.tile_pool(name="work", bufs=2))
         flip_psum = ctx.enter_context(tc.psum_pool(name="flip_psum", bufs=4))
-        feat_psum = ctx.enter_context(tc.psum_pool(name="feat_psum", bufs=2))
+        feat_psum = ctx.enter_context(tc.psum_pool(name="feat_psum", bufs=3))
         score_psum = ctx.enter_context(tc.psum_pool(name="score_psum", bufs=1))
+        ctx.enter_context(tc.manual_schedule())
 
-        w_rows = []
-        for s in range(S):
-            rows = keep.tile([P, PACK, D], BF16, name="w_rows%d" % s)
-            nc.sync.dma_start(
-                out=rows[:].rearrange("r (u e) k -> r u e k", u=HALVES),
-                in_=w_f[s * DS : (s + 1) * DS, :].rearrange("(u r e) k -> r u e k", u=HALVES, r=P),
-            )
-            w_rows.append(rows)
+        w_rows = {}
+        h_rows = {}
+        x_rows = {}
+        for k, (i, s) in enumerate(units):
             if s == 0:
+                rows = rows_pool.tile([P, D], BF16, tag="h_rows", name="h_rows%d" % i)
+                nc.sync.dma_start(out=rows[:], in_=h[i * P : (i + 1) * P, :])
+                h_rows[i] = rows
+            if i == 0:
+                slice_rows = w_f[s * DS : (s + 1) * DS, :].rearrange(
+                    "(u r e) k -> u e r k", u=HALVES, r=P
+                )
+                for t in range(PACK):
+                    rows = keep.tile([P, D], BF16, name="w_rows%d%d" % (s, t))
+                    nc.sync.dma_start(out=rows[:], in_=slice_rows[t // 2, t % 2])
+                    w_rows[(s, t)] = rows
+            if s == S - 1:
+                rows = rows_pool.tile([P, D], BF16, tag="x_rows", name="x_rows%d" % i)
+                nc.sync.dma_start(out=rows[:], in_=x2f[i * P : (i + 1) * P, :])
+                x_rows[i] = rows
+            if k == EARLY - 1:
                 vu_rows = keep.tile([P, D], BF16)
                 nc.sync.dma_start(out=vu_rows[:], in_=vu.rearrange("n s d -> n (s d)"))
-        h_rows = []
-        x_rows = []
-        for i in range(ROW_TILES):
-            rows = keep.tile([P, D], BF16, name="h_rows%d" % i)
-            nc.sync.dma_start(out=rows[:], in_=h[i * P : (i + 1) * P, :])
-            h_rows.append(rows)
-            rows = keep.tile([P, D], BF16, name="x_rows%d" % i)
-            nc.sync.dma_start(out=rows[:], in_=x2f[i * P : (i + 1) * P, :])
-            x_rows.append(rows)
 
         ident = keep.tile([P, P], F32)
         make_identity(nc, ident[:])
@@ -73,9 +95,25 @@ def tile_tpru_pa_kernel(tc, h, x2f, vu, w_f, b_f, bh, bx, out):
         bx_all = keep.tile([P, 1], F32)
         nc.vector.tensor_copy(out=bx_all[:], in_=bx_bf[:])
 
-        def pack_rows(rows, codes, scales):
+        vu_codes = keep.tile([P, S, N], U32, align_bytes=64)
+        vu_scales = keep.tile([P, S, N], U8, align_bytes=64)
+        w_codes = keep.tile([P, S, PACK, PASSES, P], U32, align_bytes=64)
+        w_scales = keep.tile([P, S, PACK, PASSES, P], U8, align_bytes=64)
+
+        flipped_at = {k: [] for k in steps}
+        h_packed = {}
+        x_packed = {}
+        feat_of = {}
+        f_grouped_of = {}
+        both_of = {}
+        f_packed = {}
+        relu_x_of = {}
+        relu_h_of = {}
+        squared_of = {}
+
+        def flip(k, rows, codes, scales, second_copy):
             words = rows.bitcast(F32)
-            grouped = stage.tile([P, PASSES, P, HALVES], F32, align_bytes=64)
+            grouped = flip_pool.tile([P, PASSES, P, HALVES], F32, align_bytes=64)
             for first in range(0, PASSES, 2):
                 flipped = flip_psum.tile([P, 2, HALVES, P], F32)
                 for g in range(2):
@@ -84,97 +122,134 @@ def tile_tpru_pa_kernel(tc, h, x2f, vu, w_f, b_f, bh, bx, out):
                         nc.tensor.transpose(
                             flipped[:, g, u, :], words[:, column : column + P], ident[:]
                         )
-                nc.scalar.copy(
+                copy = nc.scalar.copy if first == 0 else second_copy
+                copy(
                     out=grouped[:, first : first + 2, :, :],
                     in_=flipped[:].rearrange("q g u r -> q g r u"),
                 )
+            flipped_at[k].append((grouped, codes, scales))
+
+        def quantise_flipped(k):
+            for grouped, codes, scales in flipped_at.get(k, []):
+                nc.vector.quantize_mx(
+                    out=codes.rearrange("q g r -> q (g r)").bitcast(FP8X4),
+                    scales=scales.rearrange("q g r -> q (g r)"),
+                    in_=grouped[:].rearrange("q g r u -> q (g r u)").bitcast(BF16),
+                )
+
+        def flip_ahead(k):
+            ahead = k + PACK_LEAD
+            if is_unit(ahead) and units[ahead][1] == 0:
+                i = units[ahead][0]
+                h_codes = code_pool.tile([P, PASSES, P], U32, align_bytes=64)
+                h_scales = code_pool.tile([P, PASSES, P], U8, align_bytes=64)
+                flip(k, h_rows[i][:], h_codes[:], h_scales[:], nc.scalar.copy)
+                h_packed[i] = (h_codes, h_scales)
+            for u in range(HALVES):
+                ahead = k + PACK_LEAD + 1 - u
+                if is_unit(ahead) and units[ahead][0] == 0:
+                    s = units[ahead][1]
+                    t = 2 * u
+                    flip(k, w_rows[(s, t)][:], w_codes[:, s, t], w_scales[:, s, t], nc.scalar.copy)
+                    t = 2 * u + 1
+                    flip(
+                        k, w_rows[(s, t)][:], w_codes[:, s, t], w_scales[:, s, t],
+                        nc.vector.tensor_copy,
+                    )
+            ahead = k + PACK_LEAD
+            if is_unit(ahead) and units[ahead][1] == S - 1:
+                i = units[ahead][0]
+                x_codes = code_pool.tile([P, S, P], U32, align_bytes=64)
+                x_scales = code_pool.tile([P, S, P], U8, align_bytes=64)
+                flip(k, x_rows[i][:], x_codes[:], x_scales[:], nc.scalar.copy)
+                x_packed[i] = (x_codes, x_scales)
+            if k == 0:
+                flip(k, vu_rows[:], vu_codes[:], vu_scales[:], nc.scalar.copy)
+
+        def features(k):
+            i, s = units[k]
+            h_codes, h_scales = h_packed[i]
+            feat = feat_psum.tile([P, PACK, P], F32)
+            for t in range(PACK):
+                for g in range(PASSES):
+                    nc.tensor.matmul_mx(
+                        out=feat[:, t, :],
+                        lhsT=w_codes[:, s, t, g, :].bitcast(FP8X4),
+                        lhsT_scale=w_scales[:, s, t, g, :],
+                        rhs=h_codes[:, g, :].bitcast(FP8X4),
+                        rhs_scale=h_scales[:, g, :],
+                        start=(g == 0),
+                        stop=(g == PASSES - 1),
+                    )
+            feat_of[k] = feat
+
+        def add_bias(k):
+            s = units[k][1]
+            feat = feat_of[k]
+            f_grouped = feat_pool.tile([P, P, PACK], BF16, align_bytes=64)
+            nc.vector.tensor_tensor(
+                out=f_grouped[:],
+                in0=feat[:].rearrange("p t b -> p b t"),
+                in1=bias[:, s, :].unsqueeze(1).to_broadcast([P, P, PACK]),
+                op=ALU.add,
+            )
+            f_grouped_of[k] = f_grouped
+
+        def quantise_features(k):
+            f_codes = feat_pool.tile([P, P], U32, align_bytes=64)
+            f_scales = feat_pool.tile([P, P], U8, align_bytes=64)
             nc.vector.quantize_mx(
-                out=codes.rearrange("q g r -> q (g r)").bitcast(FP8X4),
-                scales=scales.rearrange("q g r -> q (g r)"),
-                in_=grouped[:].rearrange("q g r u -> q (g r u)").bitcast(BF16),
+                out=f_codes[:].bitcast(FP8X4),
+                scales=f_scales[:],
+                in_=f_grouped_of[k][:].rearrange("p b t -> p (b t)"),
+            )
+            f_packed[k] = (f_codes, f_scales)
+
+        def scores(k):
+            i, s = units[k]
+            if s == S - 1:
+                x_codes, x_scales = x_packed[i]
+                ah = flip_psum.tile([P, S, N], F32, tag="flipped")
+                for j in range(S):
+                    nc.tensor.matmul_mx(
+                        out=ah[:, j, :],
+                        lhsT=x_codes[:, j, :].bitcast(FP8X4),
+                        lhsT_scale=x_scales[:, j, :],
+                        rhs=vu_codes[:, j, :].bitcast(FP8X4),
+                        rhs_scale=vu_scales[:, j, :],
+                        start=True,
+                        stop=True,
+                    )
+                relu_h = work.tile([P, S, N], F32)
+                nc.scalar.activation(
+                    out=relu_h[:], in_=ah[:], func=ACT.Relu, bias=bh_all[:], scale=1.0
+                )
+                relu_h_of[i] = relu_h
+            if s == 0:
+                relu_x = relu_pool.tile([P, S, N], F32)
+                relu_x_of[i] = relu_x
+            f_codes, f_scales = f_packed[k]
+            ax = score_psum.tile([P, N], F32)
+            nc.tensor.matmul_mx(
+                out=ax[:],
+                lhsT=f_codes[:].bitcast(FP8X4),
+                lhsT_scale=f_scales[:],
+                rhs=vu_codes[:, s, :].bitcast(FP8X4),
+                rhs_scale=vu_scales[:, s, :],
+                start=True,
+                stop=True,
+            )
+            nc.scalar.activation(
+                out=relu_x_of[i][:, s, :], in_=ax[:], func=ACT.Relu, bias=bx_all[:], scale=1.0
             )
 
-        def pack_row_tile(i):
-            h_codes = stage.tile([P, PASSES, P], U32, align_bytes=64)
-            h_scales = stage.tile([P, PASSES, P], U8, align_bytes=64)
-            pack_rows(h_rows[i][:], h_codes[:], h_scales[:])
-            x_codes = stage.tile([P, S, P], U32, align_bytes=64)
-            x_scales = stage.tile([P, S, P], U8, align_bytes=64)
-            pack_rows(x_rows[i][:], x_codes[:], x_scales[:])
-            return h_codes, h_scales, x_codes, x_scales
-
-        vu_codes = keep.tile([P, S, N], U32, align_bytes=64)
-        vu_scales = keep.tile([P, S, N], U8, align_bytes=64)
-        w_codes = keep.tile([P, S, PACK, PASSES, P], U32, align_bytes=64)
-        w_scales = keep.tile([P, S, PACK, PASSES, P], U8, align_bytes=64)
-        for s in range(S):
-            for t in range(PACK):
-                pack_rows(w_rows[s][:, t, :], w_codes[:, s, t], w_scales[:, s, t])
-            if s == 0:
-                pack_rows(vu_rows[:], vu_codes[:], vu_scales[:])
-
-        packed = pack_row_tile(0)
-        for i in range(ROW_TILES):
-            h_codes, h_scales, x_codes, x_scales = packed
-            if i + 1 < ROW_TILES:
-                packed = pack_row_tile(i + 1)
-
-            ah = score_psum.tile([P, S, N], F32)
-            for s in range(S):
-                nc.tensor.matmul_mx(
-                    out=ah[:, s, :],
-                    lhsT=x_codes[:, s, :].bitcast(FP8X4),
-                    lhsT_scale=x_scales[:, s, :],
-                    rhs=vu_codes[:, s, :].bitcast(FP8X4),
-                    rhs_scale=vu_scales[:, s, :],
-                    start=True,
-                    stop=True,
-                )
-            relu_h = work.tile([P, S, N], F32)
-            nc.scalar.activation(out=relu_h[:], in_=ah[:], func=ACT.Relu, bias=bh_all[:], scale=1.0)
-
-            ax = score_psum.tile([P, S, N], F32)
-            for s in range(S):
-                feat = feat_psum.tile([P, PACK, P], F32)
-                for t in range(PACK):
-                    for g in range(PASSES):
-                        nc.tensor.matmul_mx(
-                            out=feat[:, t, :],
-                            lhsT=w_codes[:, s, t, g, :].bitcast(FP8X4),
-                            lhsT_scale=w_scales[:, s, t, g, :],
-                            rhs=h_codes[:, g, :].bitcast(FP8X4),
-                            rhs_scale=h_scales[:, g, :],
-                            start=(g == 0),
-                            stop=(g == PASSES - 1),
-                        )
-                f_grouped = stage.tile([P, P, PACK], BF16, align_bytes=64)
-                nc.vector.tensor_tensor(
-                    out=f_grouped[:],
-                    in0=feat[:].rearrange("p t b -> p b t"),
-                    in1=bias[:, s, :].unsqueeze(1).to_broadcast([P, P, PACK]),
-                    op=ALU.add,
-                )
-                f_codes = stage.tile([P, P], U32, align_bytes=64)
-                f_scales = stage.tile([P, P], U8, align_bytes=64)
-                nc.vector.quantize_mx(
-                    out=f_codes[:].bitcast(FP8X4),
-                    scales=f_scales[:],
-                    in_=f_grouped[:].rearrange("p b t -> p (b t)"),
-                )
-                nc.tensor.matmul_mx(
-                    out=ax[:, s, :],
-                    lhsT=f_codes[:].bitcast(FP8X4),
-                    lhsT_scale=f_scales[:],
-                    rhs=vu_codes[:, s, :].bitcast(FP8X4),
-                    rhs_scale=vu_scales[:, s, :],
-                    start=True,
-                    stop=True,
-                )
-            relu_x = work.tile([P, S, N], F32)
-            nc.scalar.activation(out=relu_x[:], in_=ax[:], func=ACT.Relu, bias=bx_all[:], scale=1.0)
-
+        def combine(i):
             both = work.tile([P, S, N], F32)
-            nc.vector.tensor_add(out=both[:], in0=relu_h[:], in1=relu_x[:])
+            nc.vector.tensor_add(out=both[:], in0=relu_h_of[i][:], in1=relu_x_of[i][:])
+            both_of[i] = both
+
+        def square(i):
+            both = both_of[i]
             squared = work.tile([P, S, N], F32)
             total = work.tile([P, S], F32)
             for s in range(S):
@@ -184,6 +259,10 @@ def tile_tpru_pa_kernel(tc, h, x2f, vu, w_f, b_f, bh, bx, out):
                     func=ACT.Square,
                     accum_out=total[:, s : s + 1],
                 )
+            squared_of[i] = (squared, total)
+
+        def normalise(i):
+            squared, total = squared_of[i]
             floored = work.tile([P, S], F32)
             nc.vector.tensor_scalar_max(out=floored[:], in0=total[:], scalar1=EPS)
             inverse = work.tile([P, S], F32)
@@ -199,3 +278,24 @@ def tile_tpru_pa_kernel(tc, h, x2f, vu, w_f, b_f, bh, bx, out):
                 out=out[i * P : (i + 1) * P].rearrange("b n s -> b (n s)"),
                 in_=share[:].rearrange("p n s -> p (n s)"),
             )
+
+        def ends_row_tile(k):
+            return is_unit(k) and units[k][1] == S - 1
+
+        for k in steps:
+            if is_unit(k):
+                features(k)
+            quantise_flipped(k - 1)
+            if ends_row_tile(k - COMBINE_LAG):
+                combine(units[k - COMBINE_LAG][0])
+            if ends_row_tile(k - NORMALISE_LAG):
+                normalise(units[k - NORMALISE_LAG][0])
+            if is_unit(k - 1):
+                quantise_features(k - 1)
+            if is_unit(k):
+                add_bias(k)
+            flip_ahead(k)
+            if is_unit(k - SCORE_LAG):
+                scores(k - SCORE_LAG)
+            if ends_row_tile(k - SQUARE_LAG):
+                square(units[k - SQUARE_LAG][0])

@@ -24,19 +24,19 @@ EPS = 1e-12
 
 FLOPS = 2 * B * D * D + 2 * (2 * B * D * N)
 
-EARLY = 3
+EARLY = 2
 PACK_LEAD = 3
 SCORE_LAG = 3
 COMBINE_LAG = 4
 SQUARE_LAG = 5
-NORMALISE_LAG = 7
+NORMALISE_LAG = 6
 
 
 def tile_tpru_pa_kernel(tc, h, x2f, vu, w_f, b_f, bh, bx, out):
     nc = tc.nc
     units = [(i, s) for s in range(S) for i in range(EARLY)]
     units += [(i, s) for i in range(EARLY, ROW_TILES) for s in range(S)]
-    steps = range(-(PACK_LEAD + 1), len(units) + NORMALISE_LAG)
+    steps = range(-PACK_LEAD, len(units) + NORMALISE_LAG)
 
     def is_unit(k):
         return 0 <= k < len(units)
@@ -45,13 +45,12 @@ def tile_tpru_pa_kernel(tc, h, x2f, vu, w_f, b_f, bh, bx, out):
         keep = ctx.enter_context(tc.tile_pool(name="keep", bufs=1))
         rows_pool = ctx.enter_context(tc.tile_pool(name="rows_pool", bufs=4))
         flip_pool = ctx.enter_context(tc.tile_pool(name="flip_pool", bufs=6))
-        code_pool = ctx.enter_context(tc.tile_pool(name="code_pool", bufs=EARLY + 1))
+        code_pool = ctx.enter_context(tc.tile_pool(name="code_pool", bufs=EARLY + 2))
         feat_pool = ctx.enter_context(tc.tile_pool(name="feat_pool", bufs=4))
         relu_pool = ctx.enter_context(tc.tile_pool(name="relu_pool", bufs=EARLY + 2))
         work = ctx.enter_context(tc.tile_pool(name="work", bufs=2))
-        flip_psum = ctx.enter_context(tc.psum_pool(name="flip_psum", bufs=4))
+        flip_psum = ctx.enter_context(tc.psum_pool(name="flip_psum", bufs=5))
         feat_psum = ctx.enter_context(tc.psum_pool(name="feat_psum", bufs=3))
-        score_psum = ctx.enter_context(tc.psum_pool(name="score_psum", bufs=1))
         ctx.enter_context(tc.manual_schedule())
 
         w_rows = {}
@@ -111,7 +110,7 @@ def tile_tpru_pa_kernel(tc, h, x2f, vu, w_f, b_f, bh, bx, out):
         relu_h_of = {}
         squared_of = {}
 
-        def flip(k, rows, codes, scales, second_copy):
+        def flip(k, rows, codes, scales):
             words = rows.bitcast(F32)
             grouped = flip_pool.tile([P, PASSES, P, HALVES], F32, align_bytes=64)
             for first in range(0, PASSES, 2):
@@ -122,8 +121,7 @@ def tile_tpru_pa_kernel(tc, h, x2f, vu, w_f, b_f, bh, bx, out):
                         nc.tensor.transpose(
                             flipped[:, g, u, :], words[:, column : column + P], ident[:]
                         )
-                copy = nc.scalar.copy if first == 0 else second_copy
-                copy(
+                nc.scalar.copy(
                     out=grouped[:, first : first + 2, :, :],
                     in_=flipped[:].rearrange("q g u r -> q g r u"),
                 )
@@ -143,28 +141,23 @@ def tile_tpru_pa_kernel(tc, h, x2f, vu, w_f, b_f, bh, bx, out):
                 i = units[ahead][0]
                 h_codes = code_pool.tile([P, PASSES, P], U32, align_bytes=64)
                 h_scales = code_pool.tile([P, PASSES, P], U8, align_bytes=64)
-                flip(k, h_rows[i][:], h_codes[:], h_scales[:], nc.scalar.copy)
+                flip(k, h_rows[i][:], h_codes[:], h_scales[:])
                 h_packed[i] = (h_codes, h_scales)
             for u in range(HALVES):
-                ahead = k + PACK_LEAD + 1 - u
+                ahead = k + PACK_LEAD - u
                 if is_unit(ahead) and units[ahead][0] == 0:
                     s = units[ahead][1]
-                    t = 2 * u
-                    flip(k, w_rows[(s, t)][:], w_codes[:, s, t], w_scales[:, s, t], nc.scalar.copy)
-                    t = 2 * u + 1
-                    flip(
-                        k, w_rows[(s, t)][:], w_codes[:, s, t], w_scales[:, s, t],
-                        nc.vector.tensor_copy,
-                    )
-            ahead = k + PACK_LEAD
+                    for t in range(2 * u, 2 * u + 2):
+                        flip(k, w_rows[(s, t)][:], w_codes[:, s, t], w_scales[:, s, t])
+            ahead = k + PACK_LEAD - 1
             if is_unit(ahead) and units[ahead][1] == S - 1:
                 i = units[ahead][0]
                 x_codes = code_pool.tile([P, S, P], U32, align_bytes=64)
                 x_scales = code_pool.tile([P, S, P], U8, align_bytes=64)
-                flip(k, x_rows[i][:], x_codes[:], x_scales[:], nc.scalar.copy)
+                flip(k, x_rows[i][:], x_codes[:], x_scales[:])
                 x_packed[i] = (x_codes, x_scales)
             if k == 0:
-                flip(k, vu_rows[:], vu_codes[:], vu_scales[:], nc.scalar.copy)
+                flip(k, vu_rows[:], vu_codes[:], vu_scales[:])
 
         def features(k):
             i, s = units[k]
@@ -229,7 +222,7 @@ def tile_tpru_pa_kernel(tc, h, x2f, vu, w_f, b_f, bh, bx, out):
                 relu_x = relu_pool.tile([P, S, N], F32)
                 relu_x_of[i] = relu_x
             f_codes, f_scales = f_packed[k]
-            ax = score_psum.tile([P, N], F32)
+            ax = flip_psum.tile([P, N], F32, tag="flipped")
             nc.tensor.matmul_mx(
                 out=ax[:],
                 lhsT=f_codes[:].bitcast(FP8X4),

@@ -74,25 +74,28 @@ def tile_tpru_pa_kernel(tc, h, x2f, vu, w_f, b_f, bh, bx, out):
                 nc.sync.dma_start(out=rows[:], in_=x2f[i * P : (i + 1) * P, :])
                 x_rows[i] = rows
             if k == EARLY - 1:
+                bias_bf = keep.tile([P, S, HALVES, 2], BF16)
+                nc.sync.dma_start(
+                    out=bias_bf[:], in_=b_f.rearrange("(s u p e) -> p s u e", s=S, u=HALVES, p=P)
+                )
+                bh_bf = keep.tile([P, 1], BF16)
+                nc.sync.dma_start(out=bh_bf[:], in_=bh.partition_broadcast(P))
+                bx_bf = keep.tile([P, 1], BF16)
+                nc.sync.dma_start(out=bx_bf[:], in_=bx.partition_broadcast(P))
+            if k == EARLY:
                 vu_rows = keep.tile([P, D], BF16)
                 nc.sync.dma_start(out=vu_rows[:], in_=vu.rearrange("n s d -> n (s d)"))
 
         ident = keep.tile([P, P], F32)
         make_identity(nc, ident[:])
-        bias_bf = keep.tile([P, S, HALVES, 2], BF16)
-        nc.scalar.dma_start(
-            out=bias_bf[:], in_=b_f.rearrange("(s u p e) -> p s u e", s=S, u=HALVES, p=P)
-        )
         bias = keep.tile([P, S, PACK], F32)
-        nc.vector.tensor_copy(out=bias[:], in_=bias_bf[:].rearrange("p s u e -> p s (u e)"))
-        bh_bf = keep.tile([P, 1], BF16)
-        nc.scalar.dma_start(out=bh_bf[:], in_=bh.partition_broadcast(P))
         bh_all = keep.tile([P, 1], F32)
-        nc.vector.tensor_copy(out=bh_all[:], in_=bh_bf[:])
-        bx_bf = keep.tile([P, 1], BF16)
-        nc.scalar.dma_start(out=bx_bf[:], in_=bx.partition_broadcast(P))
         bx_all = keep.tile([P, 1], F32)
-        nc.vector.tensor_copy(out=bx_all[:], in_=bx_bf[:])
+
+        def widen_biases():
+            nc.vector.tensor_copy(out=bias[:], in_=bias_bf[:].rearrange("p s u e -> p s (u e)"))
+            nc.vector.tensor_copy(out=bh_all[:], in_=bh_bf[:])
+            nc.vector.tensor_copy(out=bx_all[:], in_=bx_bf[:])
 
         vu_codes = keep.tile([P, S, N], U32, align_bytes=64)
         vu_scales = keep.tile([P, S, N], U8, align_bytes=64)
@@ -156,7 +159,7 @@ def tile_tpru_pa_kernel(tc, h, x2f, vu, w_f, b_f, bh, bx, out):
                 x_scales = code_pool.tile([P, S, P], U8, align_bytes=64)
                 flip(k, x_rows[i][:], x_codes[:], x_scales[:])
                 x_packed[i] = (x_codes, x_scales)
-            if k == 0:
+            if k + PACK_LEAD - 1 == SCORE_LAG:
                 flip(k, vu_rows[:], vu_codes[:], vu_scales[:])
 
         def features(k):
@@ -279,6 +282,8 @@ def tile_tpru_pa_kernel(tc, h, x2f, vu, w_f, b_f, bh, bx, out):
             if is_unit(k):
                 features(k)
             quantise_flipped(k - 1)
+            if k == 0:
+                widen_biases()
             if ends_row_tile(k - COMBINE_LAG):
                 combine(units[k - COMBINE_LAG][0])
             if ends_row_tile(k - NORMALISE_LAG):

@@ -51,7 +51,6 @@ def tile_tpru_pa_kernel(tc, h, x2f, vu, w_f, b_f, bh, bx, out):
         work = ctx.enter_context(tc.tile_pool(name="work", bufs=2))
         flip_psum = ctx.enter_context(tc.psum_pool(name="flip_psum", bufs=5))
         feat_psum = ctx.enter_context(tc.psum_pool(name="feat_psum", bufs=3))
-        ctx.enter_context(tc.manual_schedule())
 
         w_rows = {}
         h_rows = {}
@@ -74,28 +73,25 @@ def tile_tpru_pa_kernel(tc, h, x2f, vu, w_f, b_f, bh, bx, out):
                 nc.sync.dma_start(out=rows[:], in_=x2f[i * P : (i + 1) * P, :])
                 x_rows[i] = rows
             if k == EARLY - 1:
-                bias_bf = keep.tile([P, S, HALVES, 2], BF16)
-                nc.sync.dma_start(
-                    out=bias_bf[:], in_=b_f.rearrange("(s u p e) -> p s u e", s=S, u=HALVES, p=P)
-                )
-                bh_bf = keep.tile([P, 1], BF16)
-                nc.sync.dma_start(out=bh_bf[:], in_=bh.partition_broadcast(P))
-                bx_bf = keep.tile([P, 1], BF16)
-                nc.sync.dma_start(out=bx_bf[:], in_=bx.partition_broadcast(P))
-            if k == EARLY:
                 vu_rows = keep.tile([P, D], BF16)
                 nc.sync.dma_start(out=vu_rows[:], in_=vu.rearrange("n s d -> n (s d)"))
 
         ident = keep.tile([P, P], F32)
         make_identity(nc, ident[:])
+        bias_bf = keep.tile([P, S, HALVES, 2], BF16)
+        nc.scalar.dma_start(
+            out=bias_bf[:], in_=b_f.rearrange("(s u p e) -> p s u e", s=S, u=HALVES, p=P)
+        )
         bias = keep.tile([P, S, PACK], F32)
+        nc.vector.tensor_copy(out=bias[:], in_=bias_bf[:].rearrange("p s u e -> p s (u e)"))
+        bh_bf = keep.tile([P, 1], BF16)
+        nc.scalar.dma_start(out=bh_bf[:], in_=bh.partition_broadcast(P))
         bh_all = keep.tile([P, 1], F32)
+        nc.vector.tensor_copy(out=bh_all[:], in_=bh_bf[:])
+        bx_bf = keep.tile([P, 1], BF16)
+        nc.scalar.dma_start(out=bx_bf[:], in_=bx.partition_broadcast(P))
         bx_all = keep.tile([P, 1], F32)
-
-        def widen_biases():
-            nc.vector.tensor_copy(out=bias[:], in_=bias_bf[:].rearrange("p s u e -> p s (u e)"))
-            nc.vector.tensor_copy(out=bh_all[:], in_=bh_bf[:])
-            nc.vector.tensor_copy(out=bx_all[:], in_=bx_bf[:])
+        nc.vector.tensor_copy(out=bx_all[:], in_=bx_bf[:])
 
         vu_codes = keep.tile([P, S, N], U32, align_bytes=64)
         vu_scales = keep.tile([P, S, N], U8, align_bytes=64)
@@ -159,7 +155,7 @@ def tile_tpru_pa_kernel(tc, h, x2f, vu, w_f, b_f, bh, bx, out):
                 x_scales = code_pool.tile([P, S, P], U8, align_bytes=64)
                 flip(k, x_rows[i][:], x_codes[:], x_scales[:])
                 x_packed[i] = (x_codes, x_scales)
-            if k + PACK_LEAD - 1 == SCORE_LAG:
+            if k == 0:
                 flip(k, vu_rows[:], vu_codes[:], vu_scales[:])
 
         def features(k):
@@ -282,8 +278,6 @@ def tile_tpru_pa_kernel(tc, h, x2f, vu, w_f, b_f, bh, bx, out):
             if is_unit(k):
                 features(k)
             quantise_flipped(k - 1)
-            if k == 0:
-                widen_biases()
             if ends_row_tile(k - COMBINE_LAG):
                 combine(units[k - COMBINE_LAG][0])
             if ends_row_tile(k - NORMALISE_LAG):

from contextlib import ExitStack

import concourse.mybir as mybir
from concourse.masks import make_identity

F32 = mybir.dt.float32
BF16 = mybir.dt.bfloat16
U32 = mybir.dt.uint32
U8 = mybir.dt.uint8
FP8X4 = mybir.dt.float8_e4m3fn_x4
ACT = mybir.ActivationFunctionType
ALU = mybir.AluOpType

P = 128
PACK = 4
HALVES = 2
K_PASS = P * PACK

B, D, S, N = 1024, 2048, 4, 128
DS = D // S
PASSES = D // K_PASS
ROW_TILES = B // P
EPS = 1e-12

FLOPS = 2 * B * D * D + 2 * (2 * B * D * N)

EARLY = 2
PACK_LEAD = 3
SCORE_LAG = 3
COMBINE_LAG = 4
SQUARE_LAG = 5
NORMALISE_LAG = 6


def tile_tpru_pa_kernel(tc, h, x2f, vu, w_f, b_f, bh, bx, out):
    nc = tc.nc
    units = [(i, s) for s in range(S) for i in range(EARLY)]
    units += [(i, s) for i in range(EARLY, ROW_TILES) for s in range(S)]
    steps = range(-PACK_LEAD, len(units) + NORMALISE_LAG)

    def is_unit(k):
        return 0 <= k < len(units)

    with ExitStack() as ctx:
        keep = ctx.enter_context(tc.tile_pool(name="keep", bufs=1))
        rows_pool = ctx.enter_context(tc.tile_pool(name="rows_pool", bufs=4))
        flip_pool = ctx.enter_context(tc.tile_pool(name="flip_pool", bufs=6))
        code_pool = ctx.enter_context(tc.tile_pool(name="code_pool", bufs=EARLY + 2))
        feat_pool = ctx.enter_context(tc.tile_pool(name="feat_pool", bufs=4))
        relu_pool = ctx.enter_context(tc.tile_pool(name="relu_pool", bufs=EARLY + 2))
        work = ctx.enter_context(tc.tile_pool(name="work", bufs=2))
        flip_psum = ctx.enter_context(tc.psum_pool(name="flip_psum", bufs=5))
        feat_psum = ctx.enter_context(tc.psum_pool(name="feat_psum", bufs=3))

        w_rows = {}
        h_rows = {}
        x_rows = {}
        for k, (i, s) in enumerate(units):
            if s == 0:
                rows = rows_pool.tile([P, D], BF16, tag="h_rows", name="h_rows%d" % i)
                nc.sync.dma_start(out=rows[:], in_=h[i * P : (i + 1) * P, :])
                h_rows[i] = rows
            if i == 0:
                slice_rows = w_f[s * DS : (s + 1) * DS, :].rearrange(
                    "(u r e) k -> u e r k", u=HALVES, r=P
                )
                for t in range(PACK):
                    rows = keep.tile([P, D], BF16, name="w_rows%d%d" % (s, t))
                    nc.sync.dma_start(out=rows[:], in_=slice_rows[t // 2, t % 2])
                    w_rows[(s, t)] = rows
            if s == S - 1:
                rows = rows_pool.tile([P, D], BF16, tag="x_rows", name="x_rows%d" % i)
                nc.sync.dma_start(out=rows[:], in_=x2f[i * P : (i + 1) * P, :])
                x_rows[i] = rows
            if k == EARLY - 1:
                vu_rows = keep.tile([P, D], BF16)
                nc.sync.dma_start(out=vu_rows[:], in_=vu.rearrange("n s d -> n (s d)"))

        ident = keep.tile([P, P], F32)
        make_identity(nc, ident[:])
        bias_bf = keep.tile([P, S, HALVES, 2], BF16)
        nc.scalar.dma_start(
            out=bias_bf[:], in_=b_f.rearrange("(s u p e) -> p s u e", s=S, u=HALVES, p=P)
        )
        bias = keep.tile([P, S, PACK], F32)
        nc.vector.tensor_copy(out=bias[:], in_=bias_bf[:].rearrange("p s u e -> p s (u e)"))
        bh_bf = keep.tile([P, 1], BF16)
        nc.scalar.dma_start(out=bh_bf[:], in_=bh.partition_broadcast(P))
        bh_all = keep.tile([P, 1], F32)
        nc.vector.tensor_copy(out=bh_all[:], in_=bh_bf[:])
        bx_bf = keep.tile([P, 1], BF16)
        nc.scalar.dma_start(out=bx_bf[:], in_=bx.partition_broadcast(P))
        bx_all = keep.tile([P, 1], F32)
        nc.vector.tensor_copy(out=bx_all[:], in_=bx_bf[:])

        vu_codes = keep.tile([P, S, N], U32, align_bytes=64)
        vu_scales = keep.tile([P, S, N], U8, align_bytes=64)
        w_codes = keep.tile([P, S, PACK, PASSES, P], U32, align_bytes=64)
        w_scales = keep.tile([P, S, PACK, PASSES, P], U8, align_bytes=64)

        flipped_at = {k: [] for k in steps}
        h_packed = {}
        x_packed = {}
        feat_of = {}
        f_grouped_of = {}
        both_of = {}
        f_packed = {}
        relu_x_of = {}
        relu_h_of = {}
        squared_of = {}

        def flip(k, rows, codes, scales):
            words = rows.bitcast(F32)
            grouped = flip_pool.tile([P, PASSES, P, HALVES], F32, align_bytes=64)
            for first in range(0, PASSES, 2):
                flipped = flip_psum.tile([P, 2, HALVES, P], F32)
                for g in range(2):
                    for u in range(HALVES):
                        column = ((first + g) * HALVES + u) * P
                        nc.tensor.transpose(
                            flipped[:, g, u, :], words[:, column : column + P], ident[:]
                        )
                nc.scalar.copy(
                    out=grouped[:, first : first + 2, :, :],
                    in_=flipped[:].rearrange("q g u r -> q g r u"),
                )
            flipped_at[k].append((grouped, codes, scales))

        def quantise_flipped(k):
            for grouped, codes, scales in flipped_at.get(k, []):
                nc.vector.quantize_mx(
                    out=codes.rearrange("q g r -> q (g r)").bitcast(FP8X4),
                    scales=scales.rearrange("q g r -> q (g r)"),
                    in_=grouped[:].rearrange("q g r u -> q (g r u)").bitcast(BF16),
                )

        def flip_ahead(k):
            ahead = k + PACK_LEAD
            if is_unit(ahead) and units[ahead][1] == 0:
                i = units[ahead][0]
                h_codes = code_pool.tile([P, PASSES, P], U32, align_bytes=64)
                h_scales = code_pool.tile([P, PASSES, P], U8, align_bytes=64)
                flip(k, h_rows[i][:], h_codes[:], h_scales[:])
                h_packed[i] = (h_codes, h_scales)
            for u in range(HALVES):
                ahead = k + PACK_LEAD - u
                if is_unit(ahead) and units[ahead][0] == 0:
                    s = units[ahead][1]
                    for t in range(2 * u, 2 * u + 2):
                        flip(k, w_rows[(s, t)][:], w_codes[:, s, t], w_scales[:, s, t])
            ahead = k + PACK_LEAD - 1
            if is_unit(ahead) and units[ahead][1] == S - 1:
                i = units[ahead][0]
                x_codes = code_pool.tile([P, S, P], U32, align_bytes=64)
                x_scales = code_pool.tile([P, S, P], U8, align_bytes=64)
                flip(k, x_rows[i][:], x_codes[:], x_scales[:])
                x_packed[i] = (x_codes, x_scales)
            if k == 0:
                flip(k, vu_rows[:], vu_codes[:], vu_scales[:])

        def features(k):
            i, s = units[k]
            h_codes, h_scales = h_packed[i]
            feat = feat_psum.tile([P, PACK, P], F32)
            for t in range(PACK):
                for g in range(PASSES):
                    nc.tensor.matmul_mx(
                        out=feat[:, t, :],
                        lhsT=w_codes[:, s, t, g, :].bitcast(FP8X4),
                        lhsT_scale=w_scales[:, s, t, g, :],
                        rhs=h_codes[:, g, :].bitcast(FP8X4),
                        rhs_scale=h_scales[:, g, :],
                        start=(g == 0),
                        stop=(g == PASSES - 1),
                    )
            feat_of[k] = feat

        def add_bias(k):
            s = units[k][1]
            feat = feat_of[k]
            f_grouped = feat_pool.tile([P, P, PACK], BF16, align_bytes=64)
            nc.vector.tensor_tensor(
                out=f_grouped[:],
                in0=feat[:].rearrange("p t b -> p b t"),
                in1=bias[:, s, :].unsqueeze(1).to_broadcast([P, P, PACK]),
                op=ALU.add,
            )
            f_grouped_of[k] = f_grouped

        def quantise_features(k):
            f_codes = feat_pool.tile([P, P], U32, align_bytes=64)
            f_scales = feat_pool.tile([P, P], U8, align_bytes=64)
            nc.vector.quantize_mx(
                out=f_codes[:].bitcast(FP8X4),
                scales=f_scales[:],
                in_=f_grouped_of[k][:].rearrange("p b t -> p (b t)"),
            )
            f_packed[k] = (f_codes, f_scales)

        def scores(k):
            i, s = units[k]
            if s == S - 1:
                x_codes, x_scales = x_packed[i]
                ah = flip_psum.tile([P, S, N], F32, tag="flipped")
                for j in range(S):
                    nc.tensor.matmul_mx(
                        out=ah[:, j, :],
                        lhsT=x_codes[:, j, :].bitcast(FP8X4),
                        lhsT_scale=x_scales[:, j, :],
                        rhs=vu_codes[:, j, :].bitcast(FP8X4),
                        rhs_scale=vu_scales[:, j, :],
                        start=True,
                        stop=True,
                    )
                relu_h = work.tile([P, S, N], F32)
                nc.scalar.activation(
                    out=relu_h[:], in_=ah[:], func=ACT.Relu, bias=bh_all[:], scale=1.0
                )
                relu_h_of[i] = relu_h
            if s == 0:
                relu_x = relu_pool.tile([P, S, N], F32)
                relu_x_of[i] = relu_x
            f_codes, f_scales = f_packed[k]
            ax = flip_psum.tile([P, N], F32, tag="flipped")
            nc.tensor.matmul_mx(
                out=ax[:],
                lhsT=f_codes[:].bitcast(FP8X4),
                lhsT_scale=f_scales[:],
                rhs=vu_codes[:, s, :].bitcast(FP8X4),
                rhs_scale=vu_scales[:, s, :],
                start=True,
                stop=True,
            )
            nc.scalar.activation(
                out=relu_x_of[i][:, s, :], in_=ax[:], func=ACT.Relu, bias=bx_all[:], scale=1.0
            )

        def combine(i):
            both = work.tile([P, S, N], F32)
            nc.vector.tensor_add(out=both[:], in0=relu_h_of[i][:], in1=relu_x_of[i][:])
            both_of[i] = both

        def square(i):
            both = both_of[i]
            squared = work.tile([P, S, N], F32)
            total = work.tile([P, S], F32)
            for s in range(S):
                nc.scalar.activation(
                    out=squared[:, s, :],
                    in_=both[:, s, :],
                    func=ACT.Square,
                    accum_out=total[:, s : s + 1],
                )
            squared_of[i] = (squared, total)

        def normalise(i):
            squared, total = squared_of[i]
            floored = work.tile([P, S], F32)
            nc.vector.tensor_scalar_max(out=floored[:], in0=total[:], scalar1=EPS)
            inverse = work.tile([P, S], F32)
            nc.vector.reciprocal(out=inverse[:], in_=floored[:])
            share = work.tile([P, N, S], F32)
            nc.vector.tensor_tensor(
                out=share[:],
                in0=squared[:].rearrange("p s n -> p n s"),
                in1=inverse[:].unsqueeze(1).to_broadcast([P, N, S]),
                op=ALU.mult,
            )
            nc.sync.dma_start(
                out=out[i * P : (i + 1) * P].rearrange("b n s -> b (n s)"),
                in_=share[:].rearrange("p n s -> p (n s)"),
            )

        def ends_row_tile(k):
            return is_unit(k) and units[k][1] == S - 1

        for k in steps:
            if is_unit(k):
                features(k)
            quantise_flipped(k - 1)
            if ends_row_tile(k - COMBINE_LAG):
                combine(units[k - COMBINE_LAG][0])
            if ends_row_tile(k - NORMALISE_LAG):
                normalise(units[k - NORMALISE_LAG][0])
            if is_unit(k - 1):
                quantise_features(k - 1)
            if is_unit(k):
                add_bias(k)
            flip_ahead(k)
            if is_unit(k - SCORE_LAG):
                scores(k - SCORE_LAG)
            if ends_row_tile(k - SQUARE_LAG):
                square(units[k - SQUARE_LAG][0])
